import numpy as np
import ml_dtypes

BF16 = ml_dtypes.bfloat16


def bf(x):
    return np.asarray(x, np.float32).astype(BF16)


def f32(x):
    return np.asarray(x, np.float32)


def f64(x):
    return np.asarray(x).astype(np.float64)


def striped(idx):
    return np.tile(idx.reshape(-1, 16).T, (8, 1))


C, S, N, R, Q, STEP = 512, 512, 2048, 16, 127, 64
K, T = N // S, N // R


def setup_inputs():
    grid = np.random.permutation(np.resize(np.arange(-Q, Q + 1), C * S)).reshape(C, S)
    return {"table": f32(grid / STEP), "logits": f32(np.random.standard_normal((1, N))), "offs": striped(np.concatenate([np.random.permutation(S) for _ in range(K)]))}


def reference(table, logits, offs):
    idx = offs[:16].T.reshape(-1)
    e = np.exp(f64(logits).reshape(T, R))
    p = (e / e.sum(axis=-1, keepdims=True)).reshape(1, N)
    return (f64(table)[:, idx] * p).reshape(C, T, R).sum(axis=-1)

@@ -1,0 +1,54 @@
+import concourse.mybir as mybir
+
+F32 = mybir.dt.float32
+U16 = mybir.dt.uint16
+ALU = mybir.AluOpType
+X = mybir.AxisListType.X
+
+P = 128
+C, S, N, R = 512, 512, 2048, 16
+T = N // R
+BLOCKS = C // P
+PIECE = S
+PIECES = N // PIECE
+
+FLOPS = 2 * C * N
+
+
+def tile_toyl3model_kernel(tc, table, logits, offs, out):
+    nc = tc.nc
+    with tc.tile_pool(name="held", bufs=1) as held, tc.tile_pool(name="ring", bufs=2) as ring:
+        offsets = held.tile([P, N // 16], U16, name="offsets")
+        nc.sync.dma_start(offsets[:], offs)
+
+        raw = held.tile([P, T, R], F32, name="raw")
+        nc.scalar.dma_start(raw[:].rearrange("p t r -> p (t r)"), logits.broadcast_to([P, N]))
+
+        blocks = [held.tile([P, S], F32, name=f"block{b}") for b in range(BLOCKS)]
+        for b in range(BLOCKS):
+            nc.gpsimd.dma_start(blocks[b][:], table[b * P : (b + 1) * P, :])
+
+        top = held.tile([P, T], F32, name="top")
+        nc.vector.tensor_reduce(top[:], raw[:], axis=X, op=ALU.max)
+        shifted = held.tile([P, T, R], F32, name="shifted")
+        nc.vector.tensor_tensor(shifted[:], raw[:], top[:].unsqueeze(2).to_broadcast([P, T, R]), ALU.subtract)
+        grown = held.tile([P, T, R], F32, name="grown")
+        nc.scalar.activation(grown[:], shifted[:], mybir.ActivationFunctionType.Exp)
+        total = held.tile([P, T], F32, name="total")
+        nc.vector.tensor_reduce(total[:], grown[:], axis=X, op=ALU.add)
+        share = held.tile([P, T], F32, name="share")
+        nc.vector.reciprocal(share[:], total[:])
+        weights = held.tile([P, T, R], F32, name="weights")
+        nc.vector.tensor_tensor(weights[:], grown[:], share[:].unsqueeze(2).to_broadcast([P, T, R]), ALU.mult)
+        weights_flat = weights[:].rearrange("p t r -> p (t r)")
+
+        for b in range(BLOCKS):
+            weighed = ring.tile([P, T, R], F32, name="weighed")
+            weighed_flat = weighed[:].rearrange("p t r -> p (t r)")
+            for k in range(PIECES):
+                piece = slice(k * PIECE, (k + 1) * PIECE)
+                picked = blocks[b][:].indirect(offsets[:, k * PIECE // 16 : (k + 1) * PIECE // 16])
+                nc.vector.tensor_tensor(weighed_flat[:, piece], picked, weights_flat[:, piece], ALU.mult)
+            mixed = ring.tile([P, T], F32, name="mixed")
+            nc.vector.tensor_reduce(mixed[:], weighed[:], axis=X, op=ALU.add)
+            nc.sync.dma_start(out[b * P : (b + 1) * P, :], mixed[:])

@@ -1,4 +1,5 @@
 import concourse.mybir as mybir
+from concourse.masks import make_identity
 
 F32 = mybir.dt.float32
 U16 = mybir.dt.uint16
@@ -11,44 +12,71 @@ T = N // R
 BLOCKS = C // P
 PIECE = S
 PIECES = N // PIECE
+ROWS = 16
+ROW = N // ROWS
+ROW_T = ROW // R
+ROWS_A_PIECE = PIECE // ROW
 
 FLOPS = 2 * C * N
 
 
 def tile_toyl3model_kernel(tc, table, logits, offs, out):
     nc = tc.nc
-    with tc.tile_pool(name="held", bufs=1) as held, tc.tile_pool(name="ring", bufs=2) as ring:
+    with (
+        tc.tile_pool(name="held", bufs=1) as held,
+        tc.tile_pool(name="ring", bufs=2) as ring,
+        tc.psum_pool(name="psum", bufs=2) as psum,
+    ):
         offsets = held.tile([P, N // 16], U16, name="offsets")
         nc.sync.dma_start(offsets[:], offs)
 
-        raw = held.tile([P, T, R], F32, name="raw")
-        nc.scalar.dma_start(raw[:].rearrange("p t r -> p (t r)"), logits.broadcast_to([P, N]))
+        raw = held.tile([ROWS, ROW_T, R], F32, name="raw")
+        nc.scalar.dma_start(raw[:].rearrange("a t r -> a (t r)"), logits.rearrange("o (a m) -> (o a) m", a=ROWS))
 
         blocks = [held.tile([P, S], F32, name=f"block{b}") for b in range(BLOCKS)]
         for b in range(BLOCKS):
-            nc.gpsimd.dma_start(blocks[b][:], table[b * P : (b + 1) * P, :])
+            queue = nc.sync if b % 2 == 0 else nc.scalar
+            queue.dma_start(blocks[b][:], table[b * P : (b + 1) * P, :])
 
-        top = held.tile([P, T], F32, name="top")
+        identity = held.tile([P, P], F32, name="identity")
+        make_identity(nc, identity[:])
+        chosen = held.tile([ROWS, ROWS, P], F32, name="chosen")
+        nc.vector.tensor_copy(chosen[:], identity[0:ROWS, 0:ROWS].unsqueeze(2).to_broadcast([ROWS, ROWS, P]))
+
+        spread_shape = [ROWS, ROW_T, R]
+        top = held.tile([ROWS, ROW_T], F32, name="top")
         nc.vector.tensor_reduce(top[:], raw[:], axis=X, op=ALU.max)
-        shifted = held.tile([P, T, R], F32, name="shifted")
-        nc.vector.tensor_tensor(shifted[:], raw[:], top[:].unsqueeze(2).to_broadcast([P, T, R]), ALU.subtract)
-        grown = held.tile([P, T, R], F32, name="grown")
+        shifted = held.tile(spread_shape, F32, name="shifted")
+        nc.vector.tensor_tensor(shifted[:], raw[:], top[:].unsqueeze(2).to_broadcast(spread_shape), ALU.subtract)
+        grown = held.tile(spread_shape, F32, name="grown")
         nc.scalar.activation(grown[:], shifted[:], mybir.ActivationFunctionType.Exp)
-        total = held.tile([P, T], F32, name="total")
+        total = held.tile([ROWS, ROW_T], F32, name="total")
         nc.vector.tensor_reduce(total[:], grown[:], axis=X, op=ALU.add)
-        share = held.tile([P, T], F32, name="share")
+        share = held.tile([ROWS, ROW_T], F32, name="share")
         nc.vector.reciprocal(share[:], total[:])
-        weights = held.tile([P, T, R], F32, name="weights")
-        nc.vector.tensor_tensor(weights[:], grown[:], share[:].unsqueeze(2).to_broadcast([P, T, R]), ALU.mult)
-        weights_flat = weights[:].rearrange("p t r -> p (t r)")
+        soft = held.tile(spread_shape, F32, name="soft")
+        nc.vector.tensor_tensor(soft[:], grown[:], share[:].unsqueeze(2).to_broadcast(spread_shape), ALU.mult)
+        soft_rows = soft[:].rearrange("a t r -> a (t r)")
+
+        weights = [held.tile([P, PIECE], F32, name=f"weights{k}") for k in range(PIECES)]
+        for k in range(PIECES):
+            everywhere = psum.tile([P, PIECE], F32, name="everywhere")
+            for q in range(ROWS_A_PIECE):
+                nc.tensor.matmul(
+                    everywhere[:, q * ROW : (q + 1) * ROW],
+                    chosen[:, k * ROWS_A_PIECE + q, :],
+                    soft_rows,
+                    start=True,
+                    stop=True,
+                )
+            nc.scalar.copy(weights[k][:], everywhere[:])
 
         for b in range(BLOCKS):
             weighed = ring.tile([P, T, R], F32, name="weighed")
             weighed_flat = weighed[:].rearrange("p t r -> p (t r)")
             for k in range(PIECES):
-                piece = slice(k * PIECE, (k + 1) * PIECE)
                 picked = blocks[b][:].indirect(offsets[:, k * PIECE // 16 : (k + 1) * PIECE // 16])
-                nc.vector.tensor_tensor(weighed_flat[:, piece], picked, weights_flat[:, piece], ALU.mult)
+                nc.vector.tensor_tensor(weighed_flat[:, k * PIECE : (k + 1) * PIECE], picked, weights[k][:], ALU.mult)
             mixed = ring.tile([P, T], F32, name="mixed")
             nc.vector.tensor_reduce(mixed[:], weighed[:], axis=X, op=ALU.add)
             nc.sync.dma_start(out[b * P : (b + 1) * P, :], mixed[:])

@@ -77,6 +77,17 @@ def tile_toyl3model_kernel(tc, table, logits, offs, out):
             for k in range(PIECES):
                 picked = blocks[b][:].indirect(offsets[:, k * PIECE // 16 : (k + 1) * PIECE // 16])
                 nc.vector.tensor_tensor(weighed_flat[:, k * PIECE : (k + 1) * PIECE], picked, weights[k][:], ALU.mult)
+
+            sum_by_token = psum.tile([T, P], F32, name="sum_by_token")
+            for r in range(R):
+                nc.tensor.matmul(
+                    sum_by_token[:], weighed[:, :, r], identity[:], is_transpose=True, start=(r == 0), stop=(r == R - 1)
+                )
+            by_token = ring.tile([T, P], F32, name="by_token")
+            nc.scalar.copy(by_token[:], sum_by_token[:])
+
+            turned = psum.tile([P, T], F32, name="turned")
+            nc.tensor.transpose(turned[:], by_token[:], identity[:])
             mixed = ring.tile([P, T], F32, name="mixed")
-            nc.vector.tensor_reduce(mixed[:], weighed[:], axis=X, op=ALU.add)
+            nc.scalar.copy(mixed[:], turned[:])
             nc.sync.dma_start(out[b * P : (b + 1) * P, :], mixed[:])

@@ -4,6 +4,7 @@ from concourse.masks import make_identity
 F32 = mybir.dt.float32
 U16 = mybir.dt.uint16
 ALU = mybir.AluOpType
+ACT = mybir.ActivationFunctionType
 X = mybir.AxisListType.X
 
 P = 128
@@ -30,8 +31,10 @@ def tile_toyl3model_kernel(tc, table, logits, offs, out):
         offsets = held.tile([P, N // 16], U16, name="offsets")
         nc.sync.dma_start(offsets[:], offs)
 
-        raw = held.tile([ROWS, ROW_T, R], F32, name="raw")
-        nc.scalar.dma_start(raw[:].rearrange("a t r -> a (t r)"), logits.rearrange("o (a m) -> (o a) m", a=ROWS))
+        in_rows = held.tile([ROWS, ROW_T, R], F32, name="in_rows")
+        nc.scalar.dma_start(in_rows[:].rearrange("a t r -> a (t r)"), logits.rearrange("o (a m) -> (o a) m", a=ROWS))
+        by_token = held.tile([T, R], F32, name="by_token")
+        nc.scalar.dma_start(by_token[:], logits.rearrange("o (t r) -> (o t) r", r=R))
 
         blocks = [held.tile([P, S], F32, name=f"block{b}") for b in range(BLOCKS)]
         for b in range(BLOCKS):
@@ -40,39 +43,40 @@ def tile_toyl3model_kernel(tc, table, logits, offs, out):
 
         identity = held.tile([P, P], F32, name="identity")
         make_identity(nc, identity[:])
-        chosen = held.tile([ROWS, ROWS, P], F32, name="chosen")
-        nc.vector.tensor_copy(chosen[:], identity[0:ROWS, 0:ROWS].unsqueeze(2).to_broadcast([ROWS, ROWS, P]))
 
-        spread_shape = [ROWS, ROW_T, R]
+        shifted = held.tile([P, ROW_T, R], F32, name="shifted")
+        nc.gpsimd.memset(shifted[:], 0.0)
         top = held.tile([ROWS, ROW_T], F32, name="top")
-        nc.vector.tensor_reduce(top[:], raw[:], axis=X, op=ALU.max)
-        shifted = held.tile(spread_shape, F32, name="shifted")
-        nc.vector.tensor_tensor(shifted[:], raw[:], top[:].unsqueeze(2).to_broadcast(spread_shape), ALU.subtract)
-        grown = held.tile(spread_shape, F32, name="grown")
-        nc.scalar.activation(grown[:], shifted[:], mybir.ActivationFunctionType.Exp)
-        total = held.tile([ROWS, ROW_T], F32, name="total")
-        nc.vector.tensor_reduce(total[:], grown[:], axis=X, op=ALU.add)
-        share = held.tile([ROWS, ROW_T], F32, name="share")
-        nc.vector.reciprocal(share[:], total[:])
-        soft = held.tile(spread_shape, F32, name="soft")
-        nc.vector.tensor_tensor(soft[:], grown[:], share[:].unsqueeze(2).to_broadcast(spread_shape), ALU.mult)
-        soft_rows = soft[:].rearrange("a t r -> a (t r)")
+        nc.vector.tensor_reduce(top[:], in_rows[:], axis=X, op=ALU.max)
+        nc.vector.tensor_tensor(
+            shifted[0:ROWS], in_rows[:], top[:].unsqueeze(2).to_broadcast([ROWS, ROW_T, R]), ALU.subtract
+        )
+        shifted_rows = shifted[:].rearrange("a t r -> a (t r)")
 
         weights = [held.tile([P, PIECE], F32, name=f"weights{k}") for k in range(PIECES)]
         for k in range(PIECES):
             everywhere = psum.tile([P, PIECE], F32, name="everywhere")
             for q in range(ROWS_A_PIECE):
+                a = k * ROWS_A_PIECE + q
                 nc.tensor.matmul(
                     everywhere[:, q * ROW : (q + 1) * ROW],
-                    chosen[:, k * ROWS_A_PIECE + q, :],
-                    soft_rows,
+                    identity[:, a : a + 1].to_broadcast([P, P]),
+                    shifted_rows,
                     start=True,
                     stop=True,
                 )
-            nc.scalar.copy(weights[k][:], everywhere[:])
+            nc.scalar.activation(weights[k][:], everywhere[:], ACT.Exp)
+
+        minus_top = held.tile([T, 1], F32, name="minus_top")
+        nc.vector.tensor_reduce(minus_top[:], by_token[:], axis=X, op=ALU.max, negate=True)
+        grown = held.tile([T, R], F32, name="grown")
+        total = held.tile([T, 1], F32, name="total")
+        nc.scalar.activation(grown[:], by_token[:], ACT.Exp, bias=minus_top[:], accum_out=total[:])
+        share = held.tile([T, 1], F32, name="share")
+        nc.vector.reciprocal(share[:], total[:])
 
         for b in range(BLOCKS):
-            weighed = ring.tile([P, T, R], F32, name="weighed")
+            weighed = held.tile([P, T, R], F32, name=f"weighed{b}")
             weighed_flat = weighed[:].rearrange("p t r -> p (t r)")
             for k in range(PIECES):
                 picked = blocks[b][:].indirect(offsets[:, k * PIECE // 16 : (k + 1) * PIECE // 16])
@@ -83,11 +87,11 @@ def tile_toyl3model_kernel(tc, table, logits, offs, out):
                 nc.tensor.matmul(
                     sum_by_token[:], weighed[:, :, r], identity[:], is_transpose=True, start=(r == 0), stop=(r == R - 1)
                 )
-            by_token = ring.tile([T, P], F32, name="by_token")
-            nc.scalar.copy(by_token[:], sum_by_token[:])
+            mix_by_token = ring.tile([T, P], F32, name="mix_by_token")
+            nc.scalar.activation(mix_by_token[:], sum_by_token[:], ACT.Copy, scale=share[:])
 
             turned = psum.tile([P, T], F32, name="turned")
-            nc.tensor.transpose(turned[:], by_token[:], identity[:])
+            nc.tensor.transpose(turned[:], mix_by_token[:], identity[:])
             mixed = ring.tile([P, T], F32, name="mixed")
             nc.scalar.copy(mixed[:], turned[:])
             nc.sync.dma_start(out[b * P : (b + 1) * P, :], mixed[:])

@@ -27,6 +27,7 @@ def tile_toyl3model_kernel(tc, table, logits, offs, out):
         tc.tile_pool(name="held", bufs=1) as held,
         tc.tile_pool(name="ring", bufs=2) as ring,
         tc.psum_pool(name="psum", bufs=2) as psum,
+        tc.psum_pool(name="psum_held", bufs=1) as psum_held,
     ):
         offsets = held.tile([P, N // 16], U16, name="offsets")
         nc.sync.dma_start(offsets[:], offs)
@@ -75,6 +76,13 @@ def tile_toyl3model_kernel(tc, table, logits, offs, out):
         share = held.tile([T, 1], F32, name="share")
         nc.vector.reciprocal(share[:], total[:])
 
+        ones = held.tile([T, P], F32, name="ones")
+        nc.gpsimd.memset(ones[:], 1.0)
+        share_diagonal = held.tile([T, T], F32, name="share_diagonal")
+        nc.vector.tensor_scalar_mul(share_diagonal[:], identity[:], share[:])
+        share_everywhere = psum_held.tile([P, T], F32, name="share_everywhere")
+        nc.tensor.matmul(share_everywhere[:], ones[:], share_diagonal[:], start=True, stop=True)
+
         for b in range(BLOCKS):
             weighed = held.tile([P, T, R], F32, name=f"weighed{b}")
             weighed_flat = weighed[:].rearrange("p t r -> p (t r)")
@@ -82,16 +90,26 @@ def tile_toyl3model_kernel(tc, table, logits, offs, out):
                 picked = blocks[b][:].indirect(offsets[:, k * PIECE // 16 : (k + 1) * PIECE // 16])
                 nc.vector.tensor_tensor(weighed_flat[:, k * PIECE : (k + 1) * PIECE], picked, weights[k][:], ALU.mult)
 
-            sum_by_token = psum.tile([T, P], F32, name="sum_by_token")
-            for r in range(R):
-                nc.tensor.matmul(
-                    sum_by_token[:], weighed[:, :, r], identity[:], is_transpose=True, start=(r == 0), stop=(r == R - 1)
-                )
-            mix_by_token = ring.tile([T, P], F32, name="mix_by_token")
-            nc.scalar.activation(mix_by_token[:], sum_by_token[:], ACT.Copy, scale=share[:])
-
-            turned = psum.tile([P, T], F32, name="turned")
-            nc.tensor.transpose(turned[:], mix_by_token[:], identity[:])
             mixed = ring.tile([P, T], F32, name="mixed")
-            nc.scalar.copy(mixed[:], turned[:])
+            if b < BLOCKS - 1:
+                sum_by_token = psum.tile([T, P], F32, name="sum_by_token")
+                for r in range(R):
+                    nc.tensor.matmul(
+                        sum_by_token[:],
+                        weighed[:, :, r],
+                        identity[:],
+                        is_transpose=True,
+                        start=(r == 0),
+                        stop=(r == R - 1),
+                    )
+                mix_by_token = ring.tile([T, P], F32, name="mix_by_token")
+                nc.scalar.activation(mix_by_token[:], sum_by_token[:], ACT.Copy, scale=share[:])
+
+                turned = psum.tile([P, T], F32, name="turned")
+                nc.tensor.transpose(turned[:], mix_by_token[:], identity[:])
+                nc.scalar.copy(mixed[:], turned[:])
+            else:
+                sums = ring.tile([P, T], F32, name="sums")
+                nc.vector.tensor_reduce(sums[:], weighed[:], axis=X, op=ALU.add)
+                nc.vector.tensor_tensor(mixed[:], sums[:], share_everywhere[:], ALU.mult)
             nc.sync.dma_start(out[b * P : (b + 1) * P, :], mixed[:])

@@ -21,6 +21,15 @@ ROWS_A_PIECE = PIECE // ROW
 FLOPS = 2 * C * N
 
 
+def add_up_candidates(nc, psum, terms, identity):
+    sum_by_token = psum.tile([T, P], F32, name="sum_by_token")
+    for r in range(R):
+        nc.tensor.matmul(
+            sum_by_token[:], terms[:, :, r], identity[:], is_transpose=True, start=(r == 0), stop=(r == R - 1)
+        )
+    return sum_by_token
+
+
 def tile_toyl3model_kernel(tc, table, logits, offs, out):
     nc = tc.nc
     with (
@@ -34,8 +43,6 @@ def tile_toyl3model_kernel(tc, table, logits, offs, out):
 
         in_rows = held.tile([ROWS, ROW_T, R], F32, name="in_rows")
         nc.scalar.dma_start(in_rows[:].rearrange("a t r -> a (t r)"), logits.rearrange("o (a m) -> (o a) m", a=ROWS))
-        by_token = held.tile([T, R], F32, name="by_token")
-        nc.scalar.dma_start(by_token[:], logits.rearrange("o (t r) -> (o t) r", r=R))
 
         blocks = [held.tile([P, S], F32, name=f"block{b}") for b in range(BLOCKS)]
         for b in range(BLOCKS):
@@ -52,56 +59,40 @@ def tile_toyl3model_kernel(tc, table, logits, offs, out):
         nc.vector.tensor_tensor(
             shifted[0:ROWS], in_rows[:], top[:].unsqueeze(2).to_broadcast([ROWS, ROW_T, R]), ALU.subtract
         )
-        shifted_rows = shifted[:].rearrange("a t r -> a (t r)")
 
-        weights = [held.tile([P, PIECE], F32, name=f"weights{k}") for k in range(PIECES)]
+        turned_rows = psum_held.tile([ROW, P], F32, name="turned_rows")
+        nc.tensor.transpose(turned_rows[:], shifted[:].rearrange("a t r -> a (t r)"), identity[:])
+        in_columns = held.tile([ROW, ROWS], F32, name="in_columns")
+        nc.vector.tensor_copy(in_columns[:], turned_rows[:, 0:ROWS])
+
+        weights = held.tile([P, T, R], F32, name="weights")
+        weights_flat = weights[:].rearrange("p t r -> p (t r)")
         for k in range(PIECES):
             everywhere = psum.tile([P, PIECE], F32, name="everywhere")
             for q in range(ROWS_A_PIECE):
                 a = k * ROWS_A_PIECE + q
-                nc.tensor.matmul(
-                    everywhere[:, q * ROW : (q + 1) * ROW],
-                    identity[:, a : a + 1].to_broadcast([P, P]),
-                    shifted_rows,
-                    start=True,
-                    stop=True,
+                nc.tensor.transpose(
+                    everywhere[:, q * ROW : (q + 1) * ROW], in_columns[:, a : a + 1].to_broadcast([ROW, P]), identity[:]
                 )
-            nc.scalar.activation(weights[k][:], everywhere[:], ACT.Exp)
+            nc.scalar.activation(weights_flat[:, k * PIECE : (k + 1) * PIECE], everywhere[:], ACT.Exp)
 
-        minus_top = held.tile([T, 1], F32, name="minus_top")
-        nc.vector.tensor_reduce(minus_top[:], by_token[:], axis=X, op=ALU.max, negate=True)
-        grown = held.tile([T, R], F32, name="grown")
-        total = held.tile([T, 1], F32, name="total")
-        nc.scalar.activation(grown[:], by_token[:], ACT.Exp, bias=minus_top[:], accum_out=total[:])
+        total = add_up_candidates(nc, psum, weights, identity)
         share = held.tile([T, 1], F32, name="share")
-        nc.vector.reciprocal(share[:], total[:])
-
-        ones = held.tile([T, P], F32, name="ones")
-        nc.gpsimd.memset(ones[:], 1.0)
-        share_diagonal = held.tile([T, T], F32, name="share_diagonal")
-        nc.vector.tensor_scalar_mul(share_diagonal[:], identity[:], share[:])
+        nc.vector.reciprocal(share[:], total[:, 0:1])
         share_everywhere = psum_held.tile([P, T], F32, name="share_everywhere")
-        nc.tensor.matmul(share_everywhere[:], ones[:], share_diagonal[:], start=True, stop=True)
+        nc.tensor.transpose(share_everywhere[:], share[:].to_broadcast([T, P]), identity[:])
 
         for b in range(BLOCKS):
             weighed = held.tile([P, T, R], F32, name=f"weighed{b}")
             weighed_flat = weighed[:].rearrange("p t r -> p (t r)")
             for k in range(PIECES):
+                piece = slice(k * PIECE, (k + 1) * PIECE)
                 picked = blocks[b][:].indirect(offsets[:, k * PIECE // 16 : (k + 1) * PIECE // 16])
-                nc.vector.tensor_tensor(weighed_flat[:, k * PIECE : (k + 1) * PIECE], picked, weights[k][:], ALU.mult)
+                nc.vector.tensor_tensor(weighed_flat[:, piece], picked, weights_flat[:, piece], ALU.mult)
 
             mixed = ring.tile([P, T], F32, name="mixed")
             if b < BLOCKS - 1:
-                sum_by_token = psum.tile([T, P], F32, name="sum_by_token")
-                for r in range(R):
-                    nc.tensor.matmul(
-                        sum_by_token[:],
-                        weighed[:, :, r],
-                        identity[:],
-                        is_transpose=True,
-                        start=(r == 0),
-                        stop=(r == R - 1),
-                    )
+                sum_by_token = add_up_candidates(nc, psum, weighed, identity)
                 mix_by_token = ring.tile([T, P], F32, name="mix_by_token")
                 nc.scalar.activation(mix_by_token[:], sum_by_token[:], ACT.Copy, scale=share[:])
 

@@ -17,6 +17,7 @@ ROWS = 16
 ROW = N // ROWS
 ROW_T = ROW // R
 ROWS_A_PIECE = PIECE // ROW
+SHARED_T = T // 2
 
 FLOPS = 2 * C * N
 
@@ -82,25 +83,49 @@ def tile_toyl3model_kernel(tc, table, logits, offs, out):
         share_everywhere = psum_held.tile([P, T], F32, name="share_everywhere")
         nc.tensor.transpose(share_everywhere[:], share[:].to_broadcast([T, P]), identity[:])
 
-        for b in range(BLOCKS):
+        def look_up_and_weigh(b, k, products):
+            piece = slice(k * PIECE, (k + 1) * PIECE)
+            picked = blocks[b][:].indirect(offsets[:, k * PIECE // 16 : (k + 1) * PIECE // 16])
+            nc.vector.tensor_tensor(products, picked, weights_flat[:, piece], ALU.mult)
+
+        def mix_on_tensor(weighed):
+            sum_by_token = add_up_candidates(nc, psum, weighed, identity)
+            mix_by_token = ring.tile([T, P], F32, name="mix_by_token")
+            nc.scalar.activation(mix_by_token[:], sum_by_token[:], ACT.Copy, scale=share[:])
+
+            turned = psum.tile([P, T], F32, name="turned")
+            nc.tensor.transpose(turned[:], mix_by_token[:], identity[:])
+            return turned
+
+        for b in range(BLOCKS - 1):
             weighed = held.tile([P, T, R], F32, name=f"weighed{b}")
             weighed_flat = weighed[:].rearrange("p t r -> p (t r)")
             for k in range(PIECES):
-                piece = slice(k * PIECE, (k + 1) * PIECE)
-                picked = blocks[b][:].indirect(offsets[:, k * PIECE // 16 : (k + 1) * PIECE // 16])
-                nc.vector.tensor_tensor(weighed_flat[:, piece], picked, weights_flat[:, piece], ALU.mult)
-
+                look_up_and_weigh(b, k, weighed_flat[:, k * PIECE : (k + 1) * PIECE])
+            turned = mix_on_tensor(weighed)
             mixed = ring.tile([P, T], F32, name="mixed")
-            if b < BLOCKS - 1:
-                sum_by_token = add_up_candidates(nc, psum, weighed, identity)
-                mix_by_token = ring.tile([T, P], F32, name="mix_by_token")
-                nc.scalar.activation(mix_by_token[:], sum_by_token[:], ACT.Copy, scale=share[:])
-
-                turned = psum.tile([P, T], F32, name="turned")
-                nc.tensor.transpose(turned[:], mix_by_token[:], identity[:])
-                nc.scalar.copy(mixed[:], turned[:])
-            else:
-                sums = ring.tile([P, T], F32, name="sums")
-                nc.vector.tensor_reduce(sums[:], weighed[:], axis=X, op=ALU.add)
-                nc.vector.tensor_tensor(mixed[:], sums[:], share_everywhere[:], ALU.mult)
+            nc.scalar.copy(mixed[:], turned[:])
             nc.sync.dma_start(out[b * P : (b + 1) * P, :], mixed[:])
+
+        b = BLOCKS - 1
+        first = held.tile([P, T, R], F32, name="first")
+        nc.gpsimd.memset(first[:, SHARED_T:T, :], 0.0)
+        first_flat = first[:].rearrange("p t r -> p (t r)")
+        rest = held.tile([P, T - SHARED_T, R], F32, name="rest")
+        rest_flat = rest[:].rearrange("p t r -> p (t r)")
+        first_pieces = SHARED_T * R // PIECE
+        for k in range(first_pieces):
+            look_up_and_weigh(b, k, first_flat[:, k * PIECE : (k + 1) * PIECE])
+        for k in range(first_pieces, PIECES):
+            look_up_and_weigh(b, k, rest_flat[:, (k - first_pieces) * PIECE : (k - first_pieces + 1) * PIECE])
+
+        turned = mix_on_tensor(first)
+        mixed_first = held.tile([P, SHARED_T], F32, name="mixed_first")
+        nc.scalar.copy(mixed_first[:], turned[:, 0:SHARED_T])
+        nc.sync.dma_start(out[b * P : (b + 1) * P, 0:SHARED_T], mixed_first[:])
+
+        sums = held.tile([P, T - SHARED_T], F32, name="sums")
+        nc.vector.tensor_reduce(sums[:], rest[:], axis=X, op=ALU.add)
+        mixed_rest = held.tile([P, T - SHARED_T], F32, name="mixed_rest")
+        nc.vector.tensor_tensor(mixed_rest[:], sums[:], share_everywhere[:, SHARED_T:T], ALU.mult)
+        nc.sync.dma_start(out[b * P : (b + 1) * P, SHARED_T:T], mixed_rest[:])

@@ -2,6 +2,7 @@ import concourse.mybir as mybir
 from concourse.masks import make_identity
 
 F32 = mybir.dt.float32
+BF16 = mybir.dt.bfloat16
 U16 = mybir.dt.uint16
 ALU = mybir.AluOpType
 ACT = mybir.ActivationFunctionType
@@ -13,11 +14,10 @@ T = N // R
 BLOCKS = C // P
 PIECE = S
 PIECES = N // PIECE
+PIECE_T = PIECE // R
 ROWS = 16
 ROW = N // ROWS
-ROW_T = ROW // R
 ROWS_A_PIECE = PIECE // ROW
-SHARED_T = T // 2
 
 FLOPS = 2 * C * N
 
@@ -42,44 +42,64 @@ def tile_toyl3model_kernel(tc, table, logits, offs, out):
         offsets = held.tile([P, N // 16], U16, name="offsets")
         nc.sync.dma_start(offsets[:], offs)
 
-        in_rows = held.tile([ROWS, ROW_T, R], F32, name="in_rows")
-        nc.scalar.dma_start(in_rows[:].rearrange("a t r -> a (t r)"), logits.rearrange("o (a m) -> (o a) m", a=ROWS))
+        in_rows = held.tile([ROWS, ROW], F32, name="in_rows")
+        nc.scalar.dma_start(in_rows[:], logits.rearrange("o (a m) -> (o a) m", a=ROWS))
+        by_token = held.tile([T, R], F32, name="by_token")
+        nc.sync.dma_start(by_token[:], logits.rearrange("o (t r) -> (o t) r", r=R))
 
         blocks = [held.tile([P, S], F32, name=f"block{b}") for b in range(BLOCKS)]
         for b in range(BLOCKS):
             queue = nc.sync if b % 2 == 0 else nc.scalar
             queue.dma_start(blocks[b][:], table[b * P : (b + 1) * P, :])
 
+        warm = held.tile([P, 1], F32, name="warm")
+        nc.gpsimd.memset(warm[:], 0.0)
+        nc.scalar.activation(warm[:], warm[:], ACT.Exp)
+
         identity = held.tile([P, P], F32, name="identity")
         make_identity(nc, identity[:])
+        identity_bf16 = held.tile([P, P], BF16, name="identity_bf16")
+        make_identity(nc, identity_bf16[:])
 
-        shifted = held.tile([P, ROW_T, R], F32, name="shifted")
-        nc.gpsimd.memset(shifted[:], 0.0)
-        top = held.tile([ROWS, ROW_T], F32, name="top")
-        nc.vector.tensor_reduce(top[:], in_rows[:], axis=X, op=ALU.max)
-        nc.vector.tensor_tensor(
-            shifted[0:ROWS], in_rows[:], top[:].unsqueeze(2).to_broadcast([ROWS, ROW_T, R]), ALU.subtract
-        )
+        minus_top = held.tile([T, 1], BF16, name="minus_top")
+        with nc.allow_low_precision(reason="m only keeps the exponentials in range; it cancels in the division"):
+            nc.vector.tensor_reduce(minus_top[:], by_token[:], axis=X, op=ALU.max, negate=True)
 
-        turned_rows = psum_held.tile([ROW, P], F32, name="turned_rows")
-        nc.tensor.transpose(turned_rows[:], shifted[:].rearrange("a t r -> a (t r)"), identity[:])
+        turned_rows = psum_held.tile([ROW, ROWS], F32, name="turned_rows")
+        nc.tensor.matmul(turned_rows[:], in_rows[:], identity[0:ROWS, 0:ROWS], start=True, stop=True)
         in_columns = held.tile([ROW, ROWS], F32, name="in_columns")
-        nc.vector.tensor_copy(in_columns[:], turned_rows[:, 0:ROWS])
+        nc.vector.tensor_copy(in_columns[:], turned_rows[:])
 
         weights = held.tile([P, T, R], F32, name="weights")
         weights_flat = weights[:].rearrange("p t r -> p (t r)")
         for k in range(PIECES):
             everywhere = psum.tile([P, PIECE], F32, name="everywhere")
+            tokens = identity_bf16[:, k * PIECE_T : (k + 1) * PIECE_T]
+            nc.tensor.matmul(
+                everywhere[:],
+                minus_top[:].to_broadcast([T, P]),
+                tokens.unsqueeze(2).to_broadcast([T, PIECE_T, R]),
+                start=True,
+                stop=False,
+            )
             for q in range(ROWS_A_PIECE):
                 a = k * ROWS_A_PIECE + q
-                nc.tensor.transpose(
-                    everywhere[:, q * ROW : (q + 1) * ROW], in_columns[:, a : a + 1].to_broadcast([ROW, P]), identity[:]
+                nc.tensor.matmul(
+                    everywhere[:, q * ROW : (q + 1) * ROW],
+                    in_columns[:, a : a + 1].to_broadcast([ROW, P]),
+                    identity[:],
+                    is_transpose=True,
+                    start=False,
+                    stop=(q == ROWS_A_PIECE - 1),
                 )
             nc.scalar.activation(weights_flat[:, k * PIECE : (k + 1) * PIECE], everywhere[:], ACT.Exp)
 
-        total = add_up_candidates(nc, psum, weights, identity)
+        exp_by_token = held.tile([T, R], F32, name="exp_by_token")
+        total = held.tile([T, 1], F32, name="total")
+        nc.scalar.activation(exp_by_token[:], by_token[:], ACT.Exp, bias=minus_top[:], accum_out=total[:])
         share = held.tile([T, 1], F32, name="share")
-        nc.vector.reciprocal(share[:], total[:, 0:1])
+        nc.vector.reciprocal(share[:], total[:])
+
         share_everywhere = psum_held.tile([P, T], F32, name="share_everywhere")
         nc.tensor.transpose(share_everywhere[:], share[:].to_broadcast([T, P]), identity[:])
 
@@ -108,24 +128,12 @@ def tile_toyl3model_kernel(tc, table, logits, offs, out):
             nc.sync.dma_start(out[b * P : (b + 1) * P, :], mixed[:])
 
         b = BLOCKS - 1
-        first = held.tile([P, T, R], F32, name="first")
-        nc.gpsimd.memset(first[:, SHARED_T:T, :], 0.0)
-        first_flat = first[:].rearrange("p t r -> p (t r)")
-        rest = held.tile([P, T - SHARED_T, R], F32, name="rest")
-        rest_flat = rest[:].rearrange("p t r -> p (t r)")
-        first_pieces = SHARED_T * R // PIECE
-        for k in range(first_pieces):
-            look_up_and_weigh(b, k, first_flat[:, k * PIECE : (k + 1) * PIECE])
-        for k in range(first_pieces, PIECES):
-            look_up_and_weigh(b, k, rest_flat[:, (k - first_pieces) * PIECE : (k - first_pieces + 1) * PIECE])
-
-        turned = mix_on_tensor(first)
-        mixed_first = held.tile([P, SHARED_T], F32, name="mixed_first")
-        nc.scalar.copy(mixed_first[:], turned[:, 0:SHARED_T])
-        nc.sync.dma_start(out[b * P : (b + 1) * P, 0:SHARED_T], mixed_first[:])
-
-        sums = held.tile([P, T - SHARED_T], F32, name="sums")
-        nc.vector.tensor_reduce(sums[:], rest[:], axis=X, op=ALU.add)
-        mixed_rest = held.tile([P, T - SHARED_T], F32, name="mixed_rest")
-        nc.vector.tensor_tensor(mixed_rest[:], sums[:], share_everywhere[:, SHARED_T:T], ALU.mult)
-        nc.sync.dma_start(out[b * P : (b + 1) * P, SHARED_T:T], mixed_rest[:])
+        weighed = held.tile([P, T, R], F32, name=f"weighed{b}")
+        weighed_flat = weighed[:].rearrange("p t r -> p (t r)")
+        for k in range(PIECES):
+            look_up_and_weigh(b, k, weighed_flat[:, k * PIECE : (k + 1) * PIECE])
+        sums = held.tile([P, T], F32, name="sums")
+        nc.vector.tensor_reduce(sums[:], weighed[:], axis=X, op=ALU.add)
+        mixed = ring.tile([P, T], F32, name="mixed")
+        nc.vector.tensor_tensor(mixed[:], sums[:], share_everywhere[:], ALU.mult)
+        nc.sync.dma_start(out[b * P : (b + 1) * P, :], mixed[:])

@@ -14,10 +14,11 @@ T = N // R
 BLOCKS = C // P
 PIECE = S
 PIECES = N // PIECE
-PIECE_T = PIECE // R
 ROWS = 16
 ROW = N // ROWS
-ROWS_A_PIECE = PIECE // ROW
+
+PIECE_CUTS = [slice(k * PIECE, (k + 1) * PIECE) for k in range(PIECES)]
+EARLY_CUTS = [slice(0, PIECE // 2), slice(PIECE // 2, PIECE)] + PIECE_CUTS[1:]
 
 FLOPS = 2 * C * N
 
@@ -72,27 +73,27 @@ def tile_toyl3model_kernel(tc, table, logits, offs, out):
 
         weights = held.tile([P, T, R], F32, name="weights")
         weights_flat = weights[:].rearrange("p t r -> p (t r)")
-        for k in range(PIECES):
-            everywhere = psum.tile([P, PIECE], F32, name="everywhere")
-            tokens = identity_bf16[:, k * PIECE_T : (k + 1) * PIECE_T]
+        for entries in EARLY_CUTS:
+            everywhere = psum.tile([P, entries.stop - entries.start], F32, name="everywhere")
+            tokens = identity_bf16[:, entries.start // R : entries.stop // R]
             nc.tensor.matmul(
                 everywhere[:],
                 minus_top[:].to_broadcast([T, P]),
-                tokens.unsqueeze(2).to_broadcast([T, PIECE_T, R]),
+                tokens.unsqueeze(2).to_broadcast([T, tokens.shape[1], R]),
                 start=True,
                 stop=False,
             )
-            for q in range(ROWS_A_PIECE):
-                a = k * ROWS_A_PIECE + q
+            for first in range(entries.start, entries.stop, ROW):
+                a = first // ROW
                 nc.tensor.matmul(
-                    everywhere[:, q * ROW : (q + 1) * ROW],
+                    everywhere[:, first - entries.start : first - entries.start + ROW],
                     in_columns[:, a : a + 1].to_broadcast([ROW, P]),
                     identity[:],
                     is_transpose=True,
                     start=False,
-                    stop=(q == ROWS_A_PIECE - 1),
+                    stop=(first + ROW == entries.stop),
                 )
-            nc.scalar.activation(weights_flat[:, k * PIECE : (k + 1) * PIECE], everywhere[:], ACT.Exp)
+            nc.scalar.activation(weights_flat[:, entries], everywhere[:], ACT.Exp)
 
         exp_by_token = held.tile([T, R], F32, name="exp_by_token")
         total = held.tile([T, 1], F32, name="total")
@@ -103,10 +104,13 @@ def tile_toyl3model_kernel(tc, table, logits, offs, out):
         share_everywhere = psum_held.tile([P, T], F32, name="share_everywhere")
         nc.tensor.transpose(share_everywhere[:], share[:].to_broadcast([T, P]), identity[:])
 
-        def look_up_and_weigh(b, k, products):
-            piece = slice(k * PIECE, (k + 1) * PIECE)
-            picked = blocks[b][:].indirect(offsets[:, k * PIECE // 16 : (k + 1) * PIECE // 16])
-            nc.vector.tensor_tensor(products, picked, weights_flat[:, piece], ALU.mult)
+        def look_up_and_weigh(b, cuts):
+            weighed = held.tile([P, T, R], F32, name=f"weighed{b}")
+            weighed_flat = weighed[:].rearrange("p t r -> p (t r)")
+            for entries in cuts:
+                picked = blocks[b][:].indirect(offsets[:, entries.start // 16 : entries.stop // 16])
+                nc.vector.tensor_tensor(weighed_flat[:, entries], picked, weights_flat[:, entries], ALU.mult)
+            return weighed
 
         def mix_on_tensor(weighed):
             sum_by_token = add_up_candidates(nc, psum, weighed, identity)
@@ -118,20 +122,14 @@ def tile_toyl3model_kernel(tc, table, logits, offs, out):
             return turned
 
         for b in range(BLOCKS - 1):
-            weighed = held.tile([P, T, R], F32, name=f"weighed{b}")
-            weighed_flat = weighed[:].rearrange("p t r -> p (t r)")
-            for k in range(PIECES):
-                look_up_and_weigh(b, k, weighed_flat[:, k * PIECE : (k + 1) * PIECE])
+            weighed = look_up_and_weigh(b, EARLY_CUTS if b == 0 else PIECE_CUTS)
             turned = mix_on_tensor(weighed)
             mixed = ring.tile([P, T], F32, name="mixed")
             nc.scalar.copy(mixed[:], turned[:])
             nc.sync.dma_start(out[b * P : (b + 1) * P, :], mixed[:])
 
         b = BLOCKS - 1
-        weighed = held.tile([P, T, R], F32, name=f"weighed{b}")
-        weighed_flat = weighed[:].rearrange("p t r -> p (t r)")
-        for k in range(PIECES):
-            look_up_and_weigh(b, k, weighed_flat[:, k * PIECE : (k + 1) * PIECE])
+        weighed = look_up_and_weigh(b, PIECE_CUTS)
         sums = held.tile([P, T], F32, name="sums")
         nc.vector.tensor_reduce(sums[:], weighed[:], axis=X, op=ALU.add)
         mixed = ring.tile([P, T], F32, name="mixed")

@@ -103,6 +103,8 @@ def tile_toyl3model_kernel(tc, table, logits, offs, out):
 
         share_everywhere = psum_held.tile([P, T], F32, name="share_everywhere")
         nc.tensor.transpose(share_everywhere[:], share[:].to_broadcast([T, P]), identity[:])
+        share_in_sbuf = held.tile([P, T], F32, name="share_in_sbuf")
+        nc.scalar.copy(share_in_sbuf[:], share_everywhere[:])
 
         def look_up_and_weigh(b, cuts):
             weighed = held.tile([P, T, R], F32, name=f"weighed{b}")
@@ -130,8 +132,21 @@ def tile_toyl3model_kernel(tc, table, logits, offs, out):
 
         b = BLOCKS - 1
         weighed = look_up_and_weigh(b, PIECE_CUTS)
-        sums = held.tile([P, T], F32, name="sums")
-        nc.vector.tensor_reduce(sums[:], weighed[:], axis=X, op=ALU.add)
+        early_t = PIECE_CUTS[-1].start // R
+        vector_t = (early_t + T) // 2
         mixed = ring.tile([P, T], F32, name="mixed")
-        nc.vector.tensor_tensor(mixed[:], sums[:], share_everywhere[:], ALU.mult)
+
+        sums = held.tile([P, vector_t], F32, name="sums")
+        nc.vector.tensor_reduce(sums[:, 0:early_t], weighed[:, 0:early_t, :], axis=X, op=ALU.add)
+        nc.vector.tensor_reduce(sums[:, early_t:vector_t], weighed[:, early_t:vector_t, :], axis=X, op=ALU.add)
+        nc.vector.tensor_tensor(mixed[:, 0:vector_t], sums[:], share_everywhere[:, 0:vector_t], ALU.mult)
+
+        terms = weighed[:, vector_t:T, :]
+        for width in (R // 2, R // 4, R // 8, R // 16):
+            halved = held.tile([P, T - vector_t, width], F32, name=f"halved{width}")
+            nc.gpsimd.tensor_tensor(halved[:], terms[:, :, 0:width], terms[:, :, width : 2 * width], ALU.add)
+            terms = halved[:]
+        nc.gpsimd.tensor_tensor(
+            mixed[:, vector_t:T], terms.rearrange("p t r -> p (t r)"), share_in_sbuf[:, vector_t:T], ALU.mult
+        )
         nc.sync.dma_start(out[b * P : (b + 1) * P, :], mixed[:])

@@ -103,8 +103,6 @@ def tile_toyl3model_kernel(tc, table, logits, offs, out):
 
         share_everywhere = psum_held.tile([P, T], F32, name="share_everywhere")
         nc.tensor.transpose(share_everywhere[:], share[:].to_broadcast([T, P]), identity[:])
-        share_in_sbuf = held.tile([P, T], F32, name="share_in_sbuf")
-        nc.scalar.copy(share_in_sbuf[:], share_everywhere[:])
 
         def look_up_and_weigh(b, cuts):
             weighed = held.tile([P, T, R], F32, name=f"weighed{b}")
@@ -132,21 +130,15 @@ def tile_toyl3model_kernel(tc, table, logits, offs, out):
 
         b = BLOCKS - 1
         weighed = look_up_and_weigh(b, PIECE_CUTS)
-        early_t = PIECE_CUTS[-1].start // R
-        vector_t = (early_t + T) // 2
+        first_t = PIECE // R
+        last_t = T - PIECE // R
+        sums = held.tile([P, T], F32, name="sums")
         mixed = ring.tile([P, T], F32, name="mixed")
-
-        sums = held.tile([P, vector_t], F32, name="sums")
-        nc.vector.tensor_reduce(sums[:, 0:early_t], weighed[:, 0:early_t, :], axis=X, op=ALU.add)
-        nc.vector.tensor_reduce(sums[:, early_t:vector_t], weighed[:, early_t:vector_t, :], axis=X, op=ALU.add)
-        nc.vector.tensor_tensor(mixed[:, 0:vector_t], sums[:], share_everywhere[:, 0:vector_t], ALU.mult)
-
-        terms = weighed[:, vector_t:T, :]
-        for width in (R // 2, R // 4, R // 8, R // 16):
-            halved = held.tile([P, T - vector_t, width], F32, name=f"halved{width}")
-            nc.gpsimd.tensor_tensor(halved[:], terms[:, :, 0:width], terms[:, :, width : 2 * width], ALU.add)
-            terms = halved[:]
-        nc.gpsimd.tensor_tensor(
-            mixed[:, vector_t:T], terms.rearrange("p t r -> p (t r)"), share_in_sbuf[:, vector_t:T], ALU.mult
-        )
+        for t in range(first_t):
+            copied = ring.tile([P, R], F32, name="copied")
+            nc.scalar.activation(copied[:], weighed[:, t, :], ACT.Copy, accum_out=sums[:, t : t + 1])
+        for tokens in (slice(first_t, last_t), slice(last_t, T)):
+            nc.vector.tensor_reduce(sums[:, tokens], weighed[:, tokens, :], axis=X, op=ALU.add)
+        for tokens in (slice(0, last_t), slice(last_t, T)):
+            nc.vector.tensor_tensor(mixed[:, tokens], sums[:, tokens], share_everywhere[:, tokens], ALU.mult)
         nc.sync.dma_start(out[b * P : (b + 1) * P, :], mixed[:])

@@ -37,21 +37,21 @@ def tile_toyl3model_kernel(tc, table, logits, offs, out):
     with (
         tc.tile_pool(name="held", bufs=1) as held,
         tc.tile_pool(name="ring", bufs=2) as ring,
+        tc.psum_pool(name="spread", bufs=3) as spread,
         tc.psum_pool(name="psum", bufs=2) as psum,
         tc.psum_pool(name="psum_held", bufs=1) as psum_held,
     ):
-        offsets = held.tile([P, N // 16], U16, name="offsets")
-        nc.sync.dma_start(offsets[:], offs)
-
         in_rows = held.tile([ROWS, ROW], F32, name="in_rows")
-        nc.scalar.dma_start(in_rows[:], logits.rearrange("o (a m) -> (o a) m", a=ROWS))
+        nc.sync.dma_start(in_rows[:], logits.rearrange("o (a m) -> (o a) m", a=ROWS))
         by_token = held.tile([T, R], F32, name="by_token")
         nc.sync.dma_start(by_token[:], logits.rearrange("o (t r) -> (o t) r", r=R))
 
+        offsets = held.tile([P, N // 16], U16, name="offsets")
+        nc.sync.dma_start(offsets[:], offs)
+
         blocks = [held.tile([P, S], F32, name=f"block{b}") for b in range(BLOCKS)]
         for b in range(BLOCKS):
-            queue = nc.sync if b % 2 == 0 else nc.scalar
-            queue.dma_start(blocks[b][:], table[b * P : (b + 1) * P, :])
+            nc.sync.dma_start(blocks[b][:], table[b * P : (b + 1) * P, :])
 
         warm = held.tile([P, 1], F32, name="warm")
         nc.gpsimd.memset(warm[:], 0.0)
@@ -74,7 +74,7 @@ def tile_toyl3model_kernel(tc, table, logits, offs, out):
         weights = held.tile([P, T, R], F32, name="weights")
         weights_flat = weights[:].rearrange("p t r -> p (t r)")
         for entries in EARLY_CUTS:
-            everywhere = psum.tile([P, entries.stop - entries.start], F32, name="everywhere")
+            everywhere = spread.tile([P, entries.stop - entries.start], F32, name="everywhere")
             tokens = identity_bf16[:, entries.start // R : entries.stop // R]
             nc.tensor.matmul(
                 everywhere[:],
@@ -101,19 +101,19 @@ def tile_toyl3model_kernel(tc, table, logits, offs, out):
         share = held.tile([T, 1], F32, name="share")
         nc.vector.reciprocal(share[:], total[:])
 
-        share_everywhere = psum_held.tile([P, T], F32, name="share_everywhere")
+        share_everywhere = spread.tile([P, T], F32, name="share_everywhere", tag="everywhere")
         nc.tensor.transpose(share_everywhere[:], share[:].to_broadcast([T, P]), identity[:])
 
+        weighed = [held.tile([P, T, R], F32, name=f"weighed{b}") for b in range(BLOCKS)]
+
         def look_up_and_weigh(b, cuts):
-            weighed = held.tile([P, T, R], F32, name=f"weighed{b}")
-            weighed_flat = weighed[:].rearrange("p t r -> p (t r)")
             for entries in cuts:
                 picked = blocks[b][:].indirect(offsets[:, entries.start // 16 : entries.stop // 16])
-                nc.vector.tensor_tensor(weighed_flat[:, entries], picked, weights_flat[:, entries], ALU.mult)
-            return weighed
+                products = weighed[b][:].rearrange("p t r -> p (t r)")[:, entries]
+                nc.vector.tensor_tensor(products, picked, weights_flat[:, entries], ALU.mult)
 
-        def mix_on_tensor(weighed):
-            sum_by_token = add_up_candidates(nc, psum, weighed, identity)
+        def mix_on_tensor(terms):
+            sum_by_token = add_up_candidates(nc, psum, terms, identity)
             mix_by_token = ring.tile([T, P], F32, name="mix_by_token")
             nc.scalar.activation(mix_by_token[:], sum_by_token[:], ACT.Copy, scale=share[:])
 
@@ -121,24 +121,27 @@ def tile_toyl3model_kernel(tc, table, logits, offs, out):
             nc.tensor.transpose(turned[:], mix_by_token[:], identity[:])
             return turned
 
-        for b in range(BLOCKS - 1):
-            weighed = look_up_and_weigh(b, EARLY_CUTS if b == 0 else PIECE_CUTS)
-            turned = mix_on_tensor(weighed)
-            mixed = ring.tile([P, T], F32, name="mixed")
-            nc.scalar.copy(mixed[:], turned[:])
-            nc.sync.dma_start(out[b * P : (b + 1) * P, :], mixed[:])
-
-        b = BLOCKS - 1
-        weighed = look_up_and_weigh(b, PIECE_CUTS)
+        last = BLOCKS - 1
         first_t = PIECE // R
         last_t = T - PIECE // R
         sums = held.tile([P, T], F32, name="sums")
-        mixed = ring.tile([P, T], F32, name="mixed")
+        look_up_and_weigh(0, EARLY_CUTS[:2])
+        look_up_and_weigh(last, PIECE_CUTS[:1])
         for t in range(first_t):
             copied = ring.tile([P, R], F32, name="copied")
-            nc.scalar.activation(copied[:], weighed[:, t, :], ACT.Copy, accum_out=sums[:, t : t + 1])
+            nc.scalar.activation(copied[:], weighed[last][:, t, :], ACT.Copy, accum_out=sums[:, t : t + 1])
+
+        for b in range(last):
+            look_up_and_weigh(b, PIECE_CUTS if b > 0 else PIECE_CUTS[1:])
+            turned = mix_on_tensor(weighed[b])
+            mixed = ring.tile([P, T], F32, name="mixed")
+            nc.scalar.copy(mixed[:], turned[:])
+            nc.scalar.dma_start(out[b * P : (b + 1) * P, :], mixed[:])
+
+        look_up_and_weigh(last, PIECE_CUTS[1:])
+        mixed = held.tile([P, T], F32, name="last_mixed")
         for tokens in (slice(first_t, last_t), slice(last_t, T)):
-            nc.vector.tensor_reduce(sums[:, tokens], weighed[:, tokens, :], axis=X, op=ALU.add)
+            nc.vector.tensor_reduce(sums[:, tokens], weighed[last][:, tokens, :], axis=X, op=ALU.add)
         for tokens in (slice(0, last_t), slice(last_t, T)):
             nc.vector.tensor_tensor(mixed[:, tokens], sums[:, tokens], share_everywhere[:, tokens], ALU.mult)
-        nc.sync.dma_start(out[b * P : (b + 1) * P, :], mixed[:])
+        nc.sync.dma_start(out[last * P : (last + 1) * P, :], mixed[:])

@@ -18,7 +18,8 @@ ROWS = 16
 ROW = N // ROWS
 
 PIECE_CUTS = [slice(k * PIECE, (k + 1) * PIECE) for k in range(PIECES)]
-EARLY_CUTS = [slice(0, PIECE // 2), slice(PIECE // 2, PIECE)] + PIECE_CUTS[1:]
+EARLY_CUTS = [slice(0, PIECE // 2), slice(PIECE // 2, PIECE)]
+EARLY_ROWS = PIECE // 2 // ROW
 
 FLOPS = 2 * C * N
 
@@ -41,10 +42,13 @@ def tile_toyl3model_kernel(tc, table, logits, offs, out):
         tc.psum_pool(name="psum", bufs=2) as psum,
         tc.psum_pool(name="psum_held", bufs=1) as psum_held,
     ):
-        in_rows = held.tile([ROWS, ROW], F32, name="in_rows")
-        nc.sync.dma_start(in_rows[:], logits.rearrange("o (a m) -> (o a) m", a=ROWS))
         by_token = held.tile([T, R], F32, name="by_token")
         nc.sync.dma_start(by_token[:], logits.rearrange("o (t r) -> (o t) r", r=R))
+        early_columns = [held.tile([ROW, EARLY_ROWS], F32, name=f"early_columns{h}") for h in range(2)]
+        for columns, entries in zip(early_columns, EARLY_CUTS):
+            nc.sync.dma_start(columns[:], logits[0, entries].rearrange("(a j) -> j a", j=ROW))
+        in_rows = held.tile([ROWS, ROW], F32, name="in_rows")
+        nc.sync.dma_start(in_rows[:], logits.rearrange("o (a m) -> (o a) m", a=ROWS))
 
         offsets = held.tile([P, N // 16], U16, name="offsets")
         nc.sync.dma_start(offsets[:], offs)
@@ -57,23 +61,19 @@ def tile_toyl3model_kernel(tc, table, logits, offs, out):
         nc.gpsimd.memset(warm[:], 0.0)
         nc.scalar.activation(warm[:], warm[:], ACT.Exp)
 
-        identity = held.tile([P, P], F32, name="identity")
-        make_identity(nc, identity[:])
         identity_bf16 = held.tile([P, P], BF16, name="identity_bf16")
         make_identity(nc, identity_bf16[:])
+        identity = held.tile([P, P], F32, name="identity")
+        make_identity(nc, identity[:])
 
         minus_top = held.tile([T, 1], BF16, name="minus_top")
         with nc.allow_low_precision(reason="m only keeps the exponentials in range; it cancels in the division"):
             nc.vector.tensor_reduce(minus_top[:], by_token[:], axis=X, op=ALU.max, negate=True)
 
-        turned_rows = psum_held.tile([ROW, ROWS], F32, name="turned_rows")
-        nc.tensor.matmul(turned_rows[:], in_rows[:], identity[0:ROWS, 0:ROWS], start=True, stop=True)
-        in_columns = held.tile([ROW, ROWS], F32, name="in_columns")
-        nc.vector.tensor_copy(in_columns[:], turned_rows[:])
-
         weights = held.tile([P, T, R], F32, name="weights")
         weights_flat = weights[:].rearrange("p t r -> p (t r)")
-        for entries in EARLY_CUTS:
+
+        def make_weights(entries, columns):
             everywhere = spread.tile([P, entries.stop - entries.start], F32, name="everywhere")
             tokens = identity_bf16[:, entries.start // R : entries.stop // R]
             nc.tensor.matmul(
@@ -83,17 +83,27 @@ def tile_toyl3model_kernel(tc, table, logits, offs, out):
                 start=True,
                 stop=False,
             )
-            for first in range(entries.start, entries.stop, ROW):
-                a = first // ROW
+            for a in range(columns.shape[1]):
                 nc.tensor.matmul(
-                    everywhere[:, first - entries.start : first - entries.start + ROW],
-                    in_columns[:, a : a + 1].to_broadcast([ROW, P]),
+                    everywhere[:, a * ROW : (a + 1) * ROW],
+                    columns[:, a : a + 1].to_broadcast([ROW, P]),
                     identity[:],
                     is_transpose=True,
                     start=False,
-                    stop=(first + ROW == entries.stop),
+                    stop=(a == columns.shape[1] - 1),
                 )
             nc.scalar.activation(weights_flat[:, entries], everywhere[:], ACT.Exp)
+
+        for entries, columns in zip(EARLY_CUTS, early_columns):
+            make_weights(entries, columns[:])
+
+        turned_rows = psum_held.tile([ROW, ROWS], F32, name="turned_rows")
+        nc.tensor.matmul(turned_rows[:], in_rows[:], identity[0:ROWS, 0:ROWS], start=True, stop=True)
+        in_columns = held.tile([ROW, ROWS], F32, name="in_columns")
+        nc.scalar.copy(in_columns[:], turned_rows[:])
+
+        for entries in PIECE_CUTS[1:]:
+            make_weights(entries, in_columns[:, entries.start // ROW : entries.stop // ROW])
 
         exp_by_token = held.tile([T, R], F32, name="exp_by_token")
         total = held.tile([T, 1], F32, name="total")
@@ -125,7 +135,7 @@ def tile_toyl3model_kernel(tc, table, logits, offs, out):
         first_t = PIECE // R
         last_t = T - PIECE // R
         sums = held.tile([P, T], F32, name="sums")
-        look_up_and_weigh(0, EARLY_CUTS[:2])
+        look_up_and_weigh(0, EARLY_CUTS)
         look_up_and_weigh(last, PIECE_CUTS[:1])
         for t in range(first_t):
             copied = ring.tile([P, R], F32, name="copied")

@@ -14,12 +14,9 @@ T = N // R
 BLOCKS = C // P
 PIECE = S
 PIECES = N // PIECE
-ROWS = 16
-ROW = N // ROWS
 
 PIECE_CUTS = [slice(k * PIECE, (k + 1) * PIECE) for k in range(PIECES)]
-EARLY_CUTS = [slice(0, PIECE // 2), slice(PIECE // 2, PIECE)]
-EARLY_ROWS = PIECE // 2 // ROW
+CUTS = [slice(0, PIECE // 2), slice(PIECE // 2, PIECE)] + PIECE_CUTS[1:]
 
 FLOPS = 2 * C * N
 
@@ -40,15 +37,17 @@ def tile_toyl3model_kernel(tc, table, logits, offs, out):
         tc.tile_pool(name="ring", bufs=2) as ring,
         tc.psum_pool(name="spread", bufs=3) as spread,
         tc.psum_pool(name="psum", bufs=2) as psum,
-        tc.psum_pool(name="psum_held", bufs=1) as psum_held,
     ):
         by_token = held.tile([T, R], F32, name="by_token")
         nc.sync.dma_start(by_token[:], logits.rearrange("o (t r) -> (o t) r", r=R))
-        early_columns = [held.tile([ROW, EARLY_ROWS], F32, name=f"early_columns{h}") for h in range(2)]
-        for columns, entries in zip(early_columns, EARLY_CUTS):
-            nc.sync.dma_start(columns[:], logits[0, entries].rearrange("(a j) -> j a", j=ROW))
-        in_rows = held.tile([ROWS, ROW], F32, name="in_rows")
-        nc.sync.dma_start(in_rows[:], logits.rearrange("o (a m) -> (o a) m", a=ROWS))
+        columns = []
+        for half in range(2):
+            halves = held.tile([P, PIECE // 2 // P], F32, name=f"columns_of_half{half}")
+            nc.sync.dma_start(halves[:], logits[0, CUTS[half]].rearrange("(j a) -> j a", j=P))
+            columns.append(halves[:])
+        pieces = held.tile([P, PIECES - 1, PIECE // P], F32, name="columns_of_pieces")
+        nc.sync.dma_start(pieces[:], logits[0, PIECE:N].rearrange("(k j a) -> j k a", k=PIECES - 1, j=P))
+        columns += [pieces[:, k, :] for k in range(PIECES - 1)]
 
         offsets = held.tile([P, N // 16], U16, name="offsets")
         nc.sync.dma_start(offsets[:], offs)
@@ -73,7 +72,7 @@ def tile_toyl3model_kernel(tc, table, logits, offs, out):
         weights = held.tile([P, T, R], F32, name="weights")
         weights_flat = weights[:].rearrange("p t r -> p (t r)")
 
-        def make_weights(entries, columns):
+        for entries, logit in zip(CUTS, columns):
             everywhere = spread.tile([P, entries.stop - entries.start], F32, name="everywhere")
             tokens = identity_bf16[:, entries.start // R : entries.stop // R]
             nc.tensor.matmul(
@@ -83,27 +82,18 @@ def tile_toyl3model_kernel(tc, table, logits, offs, out):
                 start=True,
                 stop=False,
             )
-            for a in range(columns.shape[1]):
+            width = logit.shape[1]
+            by_column = everywhere[:].rearrange("p (j a) -> p a j", a=width)
+            for a in range(width):
                 nc.tensor.matmul(
-                    everywhere[:, a * ROW : (a + 1) * ROW],
-                    columns[:, a : a + 1].to_broadcast([ROW, P]),
+                    by_column[:, a, :],
+                    logit[:, a : a + 1].to_broadcast([P, P]),
                     identity[:],
                     is_transpose=True,
                     start=False,
-                    stop=(a == columns.shape[1] - 1),
+                    stop=(a == width - 1),
                 )
             nc.scalar.activation(weights_flat[:, entries], everywhere[:], ACT.Exp)
-
-        for entries, columns in zip(EARLY_CUTS, early_columns):
-            make_weights(entries, columns[:])
-
-        turned_rows = psum_held.tile([ROW, ROWS], F32, name="turned_rows")
-        nc.tensor.matmul(turned_rows[:], in_rows[:], identity[0:ROWS, 0:ROWS], start=True, stop=True)
-        in_columns = held.tile([ROW, ROWS], F32, name="in_columns")
-        nc.scalar.copy(in_columns[:], turned_rows[:])
-
-        for entries in PIECE_CUTS[1:]:
-            make_weights(entries, in_columns[:, entries.start // ROW : entries.stop // ROW])
 
         exp_by_token = held.tile([T, R], F32, name="exp_by_token")
         total = held.tile([T, 1], F32, name="total")
@@ -135,7 +125,7 @@ def tile_toyl3model_kernel(tc, table, logits, offs, out):
         first_t = PIECE // R
         last_t = T - PIECE // R
         sums = held.tile([P, T], F32, name="sums")
-        look_up_and_weigh(0, EARLY_CUTS)
+        look_up_and_weigh(0, CUTS[:2])
         look_up_and_weigh(last, PIECE_CUTS[:1])
         for t in range(first_t):
             copied = ring.tile([P, R], F32, name="copied")

@@ -45,15 +45,15 @@ def tile_toyl3model_kernel(tc, table, logits, offs, out):
             halves = held.tile([P, PIECE // 2 // P], F32, name=f"columns_of_half{half}")
             nc.sync.dma_start(halves[:], logits[0, CUTS[half]].rearrange("(j a) -> j a", j=P))
             columns.append(halves[:])
+        offsets = held.tile([P, N // 16], U16, name="offsets")
+        nc.sync.dma_start(offsets[:], offs)
+        blocks = [held.tile([P, S], F32, name=f"block{b}") for b in range(BLOCKS)]
+        nc.sync.dma_start(blocks[0][:], table[0:P, :])
+
         pieces = held.tile([P, PIECES - 1, PIECE // P], F32, name="columns_of_pieces")
         nc.sync.dma_start(pieces[:], logits[0, PIECE:N].rearrange("(k j a) -> j k a", k=PIECES - 1, j=P))
         columns += [pieces[:, k, :] for k in range(PIECES - 1)]
-
-        offsets = held.tile([P, N // 16], U16, name="offsets")
-        nc.sync.dma_start(offsets[:], offs)
-
-        blocks = [held.tile([P, S], F32, name=f"block{b}") for b in range(BLOCKS)]
-        for b in range(BLOCKS):
+        for b in range(1, BLOCKS):
             nc.sync.dma_start(blocks[b][:], table[b * P : (b + 1) * P, :])
 
         warm = held.tile([P, 1], F32, name="warm")
@@ -103,6 +103,8 @@ def tile_toyl3model_kernel(tc, table, logits, offs, out):
 
         share_everywhere = spread.tile([P, T], F32, name="share_everywhere", tag="everywhere")
         nc.tensor.transpose(share_everywhere[:], share[:].to_broadcast([T, P]), identity[:])
+        share_in_sbuf = held.tile([P, T], F32, name="share_in_sbuf")
+        nc.scalar.copy(share_in_sbuf[:], share_everywhere[:])
 
         weighed = [held.tile([P, T, R], F32, name=f"weighed{b}") for b in range(BLOCKS)]
 
@@ -143,5 +145,5 @@ def tile_toyl3model_kernel(tc, table, logits, offs, out):
         for tokens in (slice(first_t, last_t), slice(last_t, T)):
             nc.vector.tensor_reduce(sums[:, tokens], weighed[last][:, tokens, :], axis=X, op=ALU.add)
         for tokens in (slice(0, last_t), slice(last_t, T)):
-            nc.vector.tensor_tensor(mixed[:, tokens], sums[:, tokens], share_everywhere[:, tokens], ALU.mult)
+            nc.vector.tensor_tensor(mixed[:, tokens], sums[:, tokens], share_in_sbuf[:, tokens], ALU.mult)
         nc.sync.dma_start(out[last * P : (last + 1) * P, :], mixed[:])

import concourse.mybir as mybir
from concourse.masks import make_identity

F32 = mybir.dt.float32
BF16 = mybir.dt.bfloat16
U16 = mybir.dt.uint16
ALU = mybir.AluOpType
ACT = mybir.ActivationFunctionType
X = mybir.AxisListType.X

P = 128
C, S, N, R = 512, 512, 2048, 16
T = N // R
BLOCKS = C // P
PIECE = S
PIECES = N // PIECE

PIECE_CUTS = [slice(k * PIECE, (k + 1) * PIECE) for k in range(PIECES)]
CUTS = [slice(0, PIECE // 2), slice(PIECE // 2, PIECE)] + PIECE_CUTS[1:]

FLOPS = 2 * C * N


def add_up_candidates(nc, psum, terms, identity):
    sum_by_token = psum.tile([T, P], F32, name="sum_by_token")
    for r in range(R):
        nc.tensor.matmul(
            sum_by_token[:], terms[:, :, r], identity[:], is_transpose=True, start=(r == 0), stop=(r == R - 1)
        )
    return sum_by_token


def tile_toyl3model_kernel(tc, table, logits, offs, out):
    nc = tc.nc
    with (
        tc.tile_pool(name="held", bufs=1) as held,
        tc.tile_pool(name="ring", bufs=2) as ring,
        tc.psum_pool(name="spread", bufs=3) as spread,
        tc.psum_pool(name="psum", bufs=2) as psum,
    ):
        by_token = held.tile([T, R], F32, name="by_token")
        nc.sync.dma_start(by_token[:], logits.rearrange("o (t r) -> (o t) r", r=R))
        columns = []
        for half in range(2):
            halves = held.tile([P, PIECE // 2 // P], F32, name=f"columns_of_half{half}")
            nc.sync.dma_start(halves[:], logits[0, CUTS[half]].rearrange("(j a) -> j a", j=P))
            columns.append(halves[:])
        offsets = held.tile([P, N // 16], U16, name="offsets")
        nc.sync.dma_start(offsets[:], offs)
        blocks = [held.tile([P, S], F32, name=f"block{b}") for b in range(BLOCKS)]
        nc.sync.dma_start(blocks[0][:], table[0:P, :])

        pieces = held.tile([P, PIECES - 1, PIECE // P], F32, name="columns_of_pieces")
        nc.sync.dma_start(pieces[:], logits[0, PIECE:N].rearrange("(k j a) -> j k a", k=PIECES - 1, j=P))
        columns += [pieces[:, k, :] for k in range(PIECES - 1)]
        for b in range(1, BLOCKS):
            nc.sync.dma_start(blocks[b][:], table[b * P : (b + 1) * P, :])

        warm = held.tile([P, 1], F32, name="warm")
        nc.gpsimd.memset(warm[:], 0.0)
        nc.scalar.activation(warm[:], warm[:], ACT.Exp)

        identity_bf16 = held.tile([P, P], BF16, name="identity_bf16")
        make_identity(nc, identity_bf16[:])
        identity = held.tile([P, P], F32, name="identity")
        make_identity(nc, identity[:])

        minus_top = held.tile([T, 1], BF16, name="minus_top")
        with nc.allow_low_precision(reason="m only keeps the exponentials in range; it cancels in the division"):
            nc.vector.tensor_reduce(minus_top[:], by_token[:], axis=X, op=ALU.max, negate=True)

        weights = held.tile([P, T, R], F32, name="weights")
        weights_flat = weights[:].rearrange("p t r -> p (t r)")

        for entries, logit in zip(CUTS, columns):
            everywhere = spread.tile([P, entries.stop - entries.start], F32, name="everywhere")
            tokens = identity_bf16[:, entries.start // R : entries.stop // R]
            nc.tensor.matmul(
                everywhere[:],
                minus_top[:].to_broadcast([T, P]),
                tokens.unsqueeze(2).to_broadcast([T, tokens.shape[1], R]),
                start=True,
                stop=False,
            )
            width = logit.shape[1]
            by_column = everywhere[:].rearrange("p (j a) -> p a j", a=width)
            for a in range(width):
                nc.tensor.matmul(
                    by_column[:, a, :],
                    logit[:, a : a + 1].to_broadcast([P, P]),
                    identity[:],
                    is_transpose=True,
                    start=False,
                    stop=(a == width - 1),
                )
            nc.scalar.activation(weights_flat[:, entries], everywhere[:], ACT.Exp)

        exp_by_token = held.tile([T, R], F32, name="exp_by_token")
        total = held.tile([T, 1], F32, name="total")
        nc.scalar.activation(exp_by_token[:], by_token[:], ACT.Exp, bias=minus_top[:], accum_out=total[:])
        share = held.tile([T, 1], F32, name="share")
        nc.vector.reciprocal(share[:], total[:])

        share_everywhere = spread.tile([P, T], F32, name="share_everywhere", tag="everywhere")
        nc.tensor.transpose(share_everywhere[:], share[:].to_broadcast([T, P]), identity[:])
        share_in_sbuf = held.tile([P, T], F32, name="share_in_sbuf")
        nc.scalar.copy(share_in_sbuf[:], share_everywhere[:])

        weighed = [held.tile([P, T, R], F32, name=f"weighed{b}") for b in range(BLOCKS)]

        def look_up_and_weigh(b, cuts):
            for entries in cuts:
                picked = blocks[b][:].indirect(offsets[:, entries.start // 16 : entries.stop // 16])
                products = weighed[b][:].rearrange("p t r -> p (t r)")[:, entries]
                nc.vector.tensor_tensor(products, picked, weights_flat[:, entries], ALU.mult)

        def mix_on_tensor(terms):
            sum_by_token = add_up_candidates(nc, psum, terms, identity)
            mix_by_token = ring.tile([T, P], F32, name="mix_by_token")
            nc.scalar.activation(mix_by_token[:], sum_by_token[:], ACT.Copy, scale=share[:])

            turned = psum.tile([P, T], F32, name="turned")
            nc.tensor.transpose(turned[:], mix_by_token[:], identity[:])
            return turned

        last = BLOCKS - 1
        first_t = PIECE // R
        last_t = T - PIECE // R
        sums = held.tile([P, T], F32, name="sums")
        look_up_and_weigh(0, CUTS[:2])
        look_up_and_weigh(last, PIECE_CUTS[:1])
        for t in range(first_t):
            copied = ring.tile([P, R], F32, name="copied")
            nc.scalar.activation(copied[:], weighed[last][:, t, :], ACT.Copy, accum_out=sums[:, t : t + 1])

        for b in range(last):
            look_up_and_weigh(b, PIECE_CUTS if b > 0 else PIECE_CUTS[1:])
            turned = mix_on_tensor(weighed[b])
            mixed = ring.tile([P, T], F32, name="mixed")
            nc.scalar.copy(mixed[:], turned[:])
            nc.scalar.dma_start(out[b * P : (b + 1) * P, :], mixed[:])

        look_up_and_weigh(last, PIECE_CUTS[1:])
        mixed = held.tile([P, T], F32, name="last_mixed")
        for tokens in (slice(first_t, last_t), slice(last_t, T)):
            nc.vector.tensor_reduce(sums[:, tokens], weighed[last][:, tokens, :], axis=X, op=ALU.add)
        for tokens in (slice(0, last_t), slice(last_t, T)):
            nc.vector.tensor_tensor(mixed[:, tokens], sums[:, tokens], share_in_sbuf[:, tokens], ALU.mult)
        nc.sync.dma_start(out[last * P : (last + 1) * P, :], mixed[:])
